import numpy as np
import ml_dtypes


def mxq(x, axis, fmt="e4m3"):
    dtype, down = {"e4m3": (ml_dtypes.float8_e4m3fn, 7), "e5m2": (ml_dtypes.float8_e5m2, 14)}[fmt]
    v = np.moveaxis(np.asarray(x, np.float32).astype(ml_dtypes.bfloat16).astype(np.float64), axis, -1)
    blocks = v.reshape(v.shape[:-1] + (-1, 32))
    amax = np.abs(blocks).max(-1, keepdims=True)
    byte = np.maximum(np.where(amax > 0, np.frexp(amax)[1] - 1 + 127, 0) - down, 1)
    scale = np.exp2(byte - 127.0)
    codes = (blocks / scale).astype(np.float32).astype(dtype).astype(np.float64)
    return np.moveaxis((codes * scale).reshape(v.shape), -1, axis)


WIDE = False


def mx_kscale(k):
    if not WIDE:
        return np.ones(k)
    levels = np.array([10, -10, 5, -5, 0])
    a = np.random.permutation(np.resize(levels, k // 512 * 4)).reshape(k // 512, 4)
    idx = np.arange(k)
    return np.exp2(a[idx // 512, idx % 128 // 32])


BF16 = ml_dtypes.bfloat16


def bf(x):
    return np.asarray(x, np.float32).astype(BF16)


def f64(x):
    return np.asarray(x).astype(np.float64)


BATCH, SIZE_IN, SIZE_OUT, STEPS = 1024, 2048, 2048, 8


def _build_mask(size_in, size_out, steps):
    inp_el_counts = size_in // steps
    rows = np.arange(size_out)
    count = rows % inp_el_counts
    cols = np.arange(steps)[None, :] * inp_el_counts + count[:, None]
    mask = np.zeros((size_out, size_in), dtype=np.float32)
    mask[rows[:, None], cols] = 1.0
    return mask


def setup_inputs():
    s = mx_kscale(SIZE_IN)
    bound = np.sqrt(3.0 / STEPS)
    return {"x": bf(np.random.standard_normal((BATCH, SIZE_IN)) * s),
            "weights": bf(np.random.uniform(-bound, bound, (SIZE_OUT, SIZE_IN)) / s[None, :]),
            "bias": bf(np.random.uniform(-0.5, 0.5, SIZE_OUT)),
            "mask": bf(_build_mask(SIZE_IN, SIZE_OUT, STEPS))}


def reference(x, weights, bias, mask):
    w = f64(weights) * f64(mask)
    return (mxq(f64(x), 1, "e4m3") @ mxq(w, 1, "e4m3").T) + f64(bias)

@@ -1,0 +1,209 @@
+from contextlib import ExitStack
+
+import concourse.mybir as mybir
+from concourse.masks import make_identity
+
+F32 = mybir.dt.float32
+BF16 = mybir.dt.bfloat16
+U32 = mybir.dt.uint32
+U8 = mybir.dt.uint8
+FP8X4 = mybir.dt.float8_e4m3fn_x4
+ADD = mybir.AluOpType.add
+MULT = mybir.AluOpType.mult
+
+P = 128
+BATCH = 1024
+K = 2048
+FEAT = 2048
+FLOPS = 2 * BATCH * K * FEAT
+
+PASSES = K // 512
+ROWS = 256
+WORDS = K // 2
+N_PIECES = BATCH // ROWS
+N_CHUNKS = FEAT // ROWS
+RAW_BUFS = 10
+STORE_GROUPS = [[0, 1, 2, 3], [4, 5], [6], [7]]
+EARLY_MASK_FROM = 2
+SPLIT_MASK_TO = 2
+
+
+def tile_sparselayer_kernel(tc, x, weights, bias, mask, out):
+    nc = tc.nc
+    x_rows = x.rearrange("(p t) k -> p (t k)", t=BATCH // P)
+    out_rows = out.rearrange("(p t) n -> p t n", t=BATCH // P)
+
+    items = [("w", 0), ("x", 0), ("x", 1), ("x", 2), ("x", 3)]
+    items.extend([("w", c) for c in range(1, N_CHUNKS)])
+    group_of = {}
+    for gi, chunks in enumerate(STORE_GROUPS):
+        for c in chunks:
+            group_of[c] = gi
+
+    with ExitStack() as ctx:
+        const = ctx.enter_context(tc.tile_pool(name="const", bufs=1))
+        raw_pool = ctx.enter_context(tc.tile_pool(name="raw", bufs=RAW_BUFS))
+        grouped_pool = ctx.enter_context(tc.tile_pool(name="grouped", bufs=3))
+        wq_pool = ctx.enter_context(tc.tile_pool(name="wq", bufs=3))
+        stage_pool = ctx.enter_context(tc.tile_pool(name="stage", bufs=1))
+        tp_psum = ctx.enter_context(tc.psum_pool(name="tp", bufs=4))
+        mx_psum = ctx.enter_context(tc.psum_pool(name="mx", bufs=4))
+
+        ident = const.tile([P, P], F32)
+        make_identity(nc, ident[:])
+
+        ctx.enter_context(tc.manual_schedule())
+
+        raw = {}
+        state = {"next_load": 0, "free": RAW_BUFS}
+        bias_row = const.tile([P, FEAT], BF16)
+        nc.vector.memset(bias_row[:], 0.0)
+
+        def load_more():
+            while state["next_load"] < len(items):
+                i = state["next_load"]
+                if i == 1:
+                    nc.sync.dma_start(out=bias_row[0:1, :], in_=bias.rearrange("(o n) -> o n", o=1))
+                kind, n = items[i]
+                need = 1 if kind == "x" else 2
+                if state["free"] < need:
+                    return
+                state["free"] -= need
+                state["next_load"] += 1
+                if kind == "x":
+                    x_raw = raw_pool.tile([P, 2 * K], BF16, tag="raw")
+                    nc.sync.dma_start(out=x_raw[:], in_=x_rows[:, n * 2 * K : (n + 1) * 2 * K])
+                    raw[i] = (x_raw, None)
+                else:
+                    rows = slice(n * ROWS, (n + 1) * ROWS)
+                    w_raw = raw_pool.tile([P, 2 * K], BF16, tag="raw")
+                    nc.sync.dma_start(out=w_raw[:], in_=weights[rows, :].rearrange("(p s) k -> p (s k)", s=2))
+                    m_raw = raw_pool.tile([P, 2 * K], BF16, tag="raw")
+                    nc.sync.dma_start(out=m_raw[:], in_=mask[rows, :].rearrange("(p s) k -> p (s k)", s=2))
+                    raw[i] = (w_raw, m_raw)
+
+        load_more()
+        ones = const.tile([P, P], BF16)
+        nc.vector.memset(ones[:], 1.0)
+        bias_all = const.tile([P, FEAT], F32)
+
+        def spread_bias():
+            for b in range(FEAT // 512):
+                cols = slice(b * 512, (b + 1) * 512)
+                spread = mx_psum.tile([P, 512], F32, tag="mx")
+                nc.tensor.matmul(out=spread[:], lhsT=ones[:], rhs=bias_row[:, cols], start=True, stop=True)
+                nc.scalar.copy(out=bias_all[:, cols], in_=spread[:])
+
+        x_codes = const.tile([P, N_PIECES, PASSES * ROWS], U32, align_bytes=64)
+        x_scales = const.tile([P, N_PIECES, PASSES * ROWS], U8, align_bytes=64)
+        w_quantised = {}
+        staged = {}
+
+        def apply_mask(i):
+            kind, n = items[i]
+            if kind == "x":
+                return
+            w_raw, m_raw = raw[i]
+            if n <= SPLIT_MASK_TO:
+                w3 = w_raw[:].rearrange("p (s k) -> p s k", s=2)
+                m3 = m_raw[:].rearrange("p (s k) -> p s k", s=2)
+                for h in range(2):
+                    ks = slice(h * (K // 2), (h + 1) * (K // 2))
+                    nc.vector.tensor_tensor(out=w3[:, :, ks], in0=w3[:, :, ks], in1=m3[:, :, ks], op=MULT)
+            else:
+                nc.vector.tensor_tensor(out=w_raw[:], in0=w_raw[:], in1=m_raw[:], op=MULT)
+            state["free"] += 1
+
+        def transposes(i):
+            kind, n = items[i]
+            words = raw[i][0][:].bitcast(F32)
+            grouped = grouped_pool.tile([P, PASSES * ROWS * 4], BF16, tag="grouped", align_bytes=64)
+            grouped_words = grouped[:].bitcast(F32)
+            for g in range(PASSES):
+                bank = tp_psum.tile([P, 4, P], F32, tag="tp")
+                for s in range(2):
+                    for u in range(2):
+                        first = s * WORDS + (2 * g + u) * P
+                        nc.tensor.transpose(out=bank[:, 2 * s + u, :], in_=words[:, first : first + P], identity=ident[:])
+                dst = grouped_words[:, g * 2 * ROWS : (g + 1) * 2 * ROWS]
+                if kind == "x":
+                    dst = dst.rearrange("p (s j u) -> p s j u", s=2, u=2)
+                    src = bank[:].rearrange("p (s u) j -> p s j u", s=2)
+                    if g == PASSES - 1:
+                        nc.vector.tensor_copy(out=dst, in_=src)
+                    else:
+                        nc.scalar.copy(out=dst, in_=src)
+                else:
+                    nc.scalar.copy(out=dst.rearrange("p (j q) -> p j q", q=4), in_=bank[:].rearrange("p q j -> p j q"))
+            state["free"] += 1
+            return grouped
+
+        def quantise(i, grouped):
+            kind, n = items[i]
+            if kind == "x":
+                codes = x_codes[:, n, :]
+                scales = x_scales[:, n, :]
+            else:
+                w_codes = wq_pool.tile([P, PASSES * ROWS], U32, tag="w_codes", align_bytes=64)
+                w_scales = wq_pool.tile([P, PASSES * ROWS], U8, tag="w_scales", align_bytes=64)
+                w_quantised[n] = (w_codes, w_scales)
+                codes = w_codes[:]
+                scales = w_scales[:]
+            nc.vector.quantize_mx(out=codes.bitcast(FP8X4), scales=scales, in_=grouped[:])
+
+        def cell(c, tp):
+            w_codes, w_scales = w_quantised[c]
+            acc = mx_psum.tile([P, 2, ROWS], F32, tag="mx")
+            for tt in range(2):
+                for g in range(PASSES):
+                    xs = slice((2 * g + tt) * P, (2 * g + tt + 1) * P)
+                    ws = slice(g * ROWS, (g + 1) * ROWS)
+                    nc.tensor.matmul_mx(
+                        out=acc[:, tt, :],
+                        lhsT=x_codes[:, tp, xs].bitcast(FP8X4),
+                        lhsT_scale=x_scales[:, tp, xs],
+                        rhs=w_codes[:, ws].bitcast(FP8X4),
+                        rhs_scale=w_scales[:, ws],
+                        start=(g == 0),
+                        stop=(g == PASSES - 1),
+                    )
+            gi = group_of[c]
+            chunks = STORE_GROUPS[gi]
+            part = c - chunks[0]
+            width = len(chunks) * ROWS
+            if (gi, tp) not in staged:
+                result = stage_pool.tile([P, 2, width], F32, name="result_%d_%d" % (gi, tp))
+                staged[(gi, tp)] = result
+            result = staged[(gi, tp)]
+            bias_cols = bias_all[:, c * ROWS : (c + 1) * ROWS].unsqueeze(1).to_broadcast([P, 2, ROWS])
+            nc.vector.tensor_tensor(out=result[:, :, part * ROWS : (part + 1) * ROWS], in0=acc[:], in1=bias_cols, op=ADD)
+            if c == chunks[-1]:
+                first = chunks[0] * ROWS
+                nc.sync.dma_start(out=out_rows[:, 2 * tp : 2 * tp + 2, first : first + width], in_=result[:])
+
+        def is_early(i):
+            return i < len(items) and items[i][0] == "w" and items[i][1] >= EARLY_MASK_FROM
+
+        have = {"x": [], "w": []}
+        pending = []
+        apply_mask(0)
+        for i in range(len(items)):
+            if is_early(i + 1):
+                apply_mask(i + 1)
+            grouped = transposes(i)
+            load_more()
+            quantise(i, grouped)
+            if i == 1:
+                spread_bias()
+            for c, tp in pending:
+                cell(c, tp)
+            if i + 1 < len(items) and not is_early(i + 1):
+                apply_mask(i + 1)
+            kind, n = items[i]
+            if kind == "x":
+                pending = [(c, n) for c in have["w"]]
+            else:
+                pending = [(n, tp) for tp in have["x"]]
+            have[kind].append(n)
+        for c, tp in pending:
+            cell(c, tp)

@@ -52,7 +52,6 @@ def tile_sparselayer_kernel(tc, x, weights, bias, mask, out):
         ident = const.tile([P, P], F32)
         make_identity(nc, ident[:])
 
-        ctx.enter_context(tc.manual_schedule())
 
         raw = {}
         state = {"next_load": 0, "free": RAW_BUFS}

@@ -22,10 +22,18 @@ ROWS = 256
 WORDS = K // 2
 N_PIECES = BATCH // ROWS
 N_CHUNKS = FEAT // ROWS
-RAW_BUFS = 10
+RAW_BUFS = 8
+HALF_BUFS = 8
+HALF_CHUNKS = 3
+NARROW = [1, 2]
+FINE_TO = 3
+AHEAD_FROM = 1
+LAG = 1
+X_VECTOR_BANKS = [3]
 STORE_GROUPS = [[0, 1, 2, 3], [4, 5], [6], [7]]
-EARLY_MASK_FROM = 2
-SPLIT_MASK_TO = 2
+BIAS_AT = {0: [0, 1, 2, 3]}
+BIAS_VECTOR = []
+WHOLE = 2
 
 
 def tile_sparselayer_kernel(tc, x, weights, bias, mask, out):
@@ -33,8 +41,14 @@ def tile_sparselayer_kernel(tc, x, weights, bias, mask, out):
     x_rows = x.rearrange("(p t) k -> p (t k)", t=BATCH // P)
     out_rows = out.rearrange("(p t) n -> p t n", t=BATCH // P)
 
-    items = [("w", 0), ("x", 0), ("x", 1), ("x", 2), ("x", 3)]
-    items.extend([("w", c) for c in range(1, N_CHUNKS)])
+    def w_units(c):
+        if c < HALF_CHUNKS:
+            return [("w", c, 0), ("w", c, 1)]
+        return [("w", c, WHOLE)]
+
+    units = w_units(0) + [("x", tp, WHOLE) for tp in range(N_PIECES)]
+    for c in range(1, N_CHUNKS):
+        units.extend(w_units(c))
     group_of = {}
     for gi, chunks in enumerate(STORE_GROUPS):
         for c in chunks:
@@ -43,7 +57,8 @@ def tile_sparselayer_kernel(tc, x, weights, bias, mask, out):
     with ExitStack() as ctx:
         const = ctx.enter_context(tc.tile_pool(name="const", bufs=1))
         raw_pool = ctx.enter_context(tc.tile_pool(name="raw", bufs=RAW_BUFS))
-        grouped_pool = ctx.enter_context(tc.tile_pool(name="grouped", bufs=3))
+        half_pool = ctx.enter_context(tc.tile_pool(name="half", bufs=HALF_BUFS))
+        grouped_pool = ctx.enter_context(tc.tile_pool(name="grouped", bufs=2))
         wq_pool = ctx.enter_context(tc.tile_pool(name="wq", bufs=3))
         stage_pool = ctx.enter_context(tc.tile_pool(name="stage", bufs=1))
         tp_psum = ctx.enter_context(tc.psum_pool(name="tp", bufs=4))
@@ -52,33 +67,42 @@ def tile_sparselayer_kernel(tc, x, weights, bias, mask, out):
         ident = const.tile([P, P], F32)
         make_identity(nc, ident[:])
 
+        ctx.enter_context(tc.manual_schedule())
 
         raw = {}
-        state = {"next_load": 0, "free": RAW_BUFS}
+        state = {"next_load": 0, "raw": RAW_BUFS, "half": HALF_BUFS}
         bias_row = const.tile([P, FEAT], BF16)
         nc.vector.memset(bias_row[:], 0.0)
 
         def load_more():
-            while state["next_load"] < len(items):
+            while state["next_load"] < len(units):
                 i = state["next_load"]
+                kind, n, h = units[i]
+                pool_name = "raw" if h == WHOLE else "half"
+                need = 1 if kind == "x" else 2
+                if state[pool_name] < need:
+                    return
+                state[pool_name] -= need
+                state["next_load"] += 1
                 if i == 1:
                     nc.sync.dma_start(out=bias_row[0:1, :], in_=bias.rearrange("(o n) -> o n", o=1))
-                kind, n = items[i]
-                need = 1 if kind == "x" else 2
-                if state["free"] < need:
-                    return
-                state["free"] -= need
-                state["next_load"] += 1
                 if kind == "x":
                     x_raw = raw_pool.tile([P, 2 * K], BF16, tag="raw")
                     nc.sync.dma_start(out=x_raw[:], in_=x_rows[:, n * 2 * K : (n + 1) * 2 * K])
                     raw[i] = (x_raw, None)
-                else:
+                elif h == WHOLE:
                     rows = slice(n * ROWS, (n + 1) * ROWS)
                     w_raw = raw_pool.tile([P, 2 * K], BF16, tag="raw")
                     nc.sync.dma_start(out=w_raw[:], in_=weights[rows, :].rearrange("(p s) k -> p (s k)", s=2))
                     m_raw = raw_pool.tile([P, 2 * K], BF16, tag="raw")
                     nc.sync.dma_start(out=m_raw[:], in_=mask[rows, :].rearrange("(p s) k -> p (s k)", s=2))
+                    raw[i] = (w_raw, m_raw)
+                else:
+                    rows = slice(n * ROWS + h * P, n * ROWS + (h + 1) * P)
+                    w_raw = half_pool.tile([P, K], BF16, tag="half")
+                    nc.sync.dma_start(out=w_raw[:], in_=weights[rows, :])
+                    m_raw = half_pool.tile([P, K], BF16, tag="half")
+                    nc.sync.dma_start(out=m_raw[:], in_=mask[rows, :])
                     raw[i] = (w_raw, m_raw)
 
         load_more()
@@ -86,123 +110,183 @@ def tile_sparselayer_kernel(tc, x, weights, bias, mask, out):
         nc.vector.memset(ones[:], 1.0)
         bias_all = const.tile([P, FEAT], F32)
 
-        def spread_bias():
-            for b in range(FEAT // 512):
-                cols = slice(b * 512, (b + 1) * 512)
-                spread = mx_psum.tile([P, 512], F32, tag="mx")
-                nc.tensor.matmul(out=spread[:], lhsT=ones[:], rhs=bias_row[:, cols], start=True, stop=True)
+        def spread_bias(b):
+            cols = slice(b * 512, (b + 1) * 512)
+            spread = mx_psum.tile([P, 512], F32, tag="mx")
+            nc.tensor.matmul(out=spread[:], lhsT=ones[:], rhs=bias_row[:, cols], start=True, stop=True)
+            if b in BIAS_VECTOR:
+                nc.vector.tensor_copy(out=bias_all[:, cols], in_=spread[:])
+            else:
                 nc.scalar.copy(out=bias_all[:, cols], in_=spread[:])
 
         x_codes = const.tile([P, N_PIECES, PASSES * ROWS], U32, align_bytes=64)
         x_scales = const.tile([P, N_PIECES, PASSES * ROWS], U8, align_bytes=64)
         w_quantised = {}
+        grouped_of = {}
         staged = {}
+        banks_open = {}
+        mask_parts = {}
 
-        def apply_mask(i):
-            kind, n = items[i]
-            if kind == "x":
+        def n_banks(i):
+            return 4 if units[i][2] == WHOLE else 2
+
+        def is_fine(i):
+            kind, n, h = units[i]
+            return kind == "x" or n <= FINE_TO
+
+        def pool_of(i):
+            return "raw" if units[i][2] == WHOLE else "half"
+
+        for i in range(len(units)):
+            if units[i][0] == "w":
+                mask_parts[i] = n_banks(i) if is_fine(i) else 1
+
+        def apply_mask(i, count):
+            if i >= len(units) or units[i][0] == "x":
                 return
+            kind, n, h = units[i]
             w_raw, m_raw = raw[i]
-            if n <= SPLIT_MASK_TO:
-                w3 = w_raw[:].rearrange("p (s k) -> p s k", s=2)
-                m3 = m_raw[:].rearrange("p (s k) -> p s k", s=2)
-                for h in range(2):
-                    ks = slice(h * (K // 2), (h + 1) * (K // 2))
+            for r in range(count):
+                if mask_parts[i] == 0:
+                    return
+                b = n_banks(i) - mask_parts[i]
+                mask_parts[i] -= 1
+                if not is_fine(i):
+                    nc.vector.tensor_tensor(out=w_raw[:], in0=w_raw[:], in1=m_raw[:], op=MULT)
+                elif h == WHOLE:
+                    ks = slice(b * 512, (b + 1) * 512)
+                    w3 = w_raw[:].rearrange("p (s k) -> p s k", s=2)
+                    m3 = m_raw[:].rearrange("p (s k) -> p s k", s=2)
                     nc.vector.tensor_tensor(out=w3[:, :, ks], in0=w3[:, :, ks], in1=m3[:, :, ks], op=MULT)
-            else:
-                nc.vector.tensor_tensor(out=w_raw[:], in0=w_raw[:], in1=m_raw[:], op=MULT)
-            state["free"] += 1
-
-        def transposes(i):
-            kind, n = items[i]
-            words = raw[i][0][:].bitcast(F32)
-            grouped = grouped_pool.tile([P, PASSES * ROWS * 4], BF16, tag="grouped", align_bytes=64)
-            grouped_words = grouped[:].bitcast(F32)
-            for g in range(PASSES):
-                bank = tp_psum.tile([P, 4, P], F32, tag="tp")
-                for s in range(2):
-                    for u in range(2):
-                        first = s * WORDS + (2 * g + u) * P
-                        nc.tensor.transpose(out=bank[:, 2 * s + u, :], in_=words[:, first : first + P], identity=ident[:])
-                dst = grouped_words[:, g * 2 * ROWS : (g + 1) * 2 * ROWS]
-                if kind == "x":
-                    dst = dst.rearrange("p (s j u) -> p s j u", s=2, u=2)
-                    src = bank[:].rearrange("p (s u) j -> p s j u", s=2)
-                    if g == PASSES - 1:
-                        nc.vector.tensor_copy(out=dst, in_=src)
-                    else:
-                        nc.scalar.copy(out=dst, in_=src)
                 else:
-                    nc.scalar.copy(out=dst.rearrange("p (j q) -> p j q", q=4), in_=bank[:].rearrange("p q j -> p j q"))
-            state["free"] += 1
-            return grouped
+                    ks = slice(b * 1024, (b + 1) * 1024)
+                    nc.vector.tensor_tensor(out=w_raw[:, ks], in0=w_raw[:, ks], in1=m_raw[:, ks], op=MULT)
+                if mask_parts[i] == 0:
+                    state[pool_of(i)] += 1
 
-        def quantise(i, grouped):
-            kind, n = items[i]
-            if kind == "x":
-                codes = x_codes[:, n, :]
-                scales = x_scales[:, n, :]
+        def fill_bank(i, b):
+            kind, n, h = units[i]
+            words = raw[i][0][:].bitcast(F32)
+            bank = tp_psum.tile([P, 4, P], F32, tag="tp")
+            for q in range(4):
+                if h == WHOLE:
+                    first = (q // 2) * WORDS + (2 * b + q % 2) * P
+                else:
+                    first = (4 * b + q) * P
+                nc.tensor.transpose(out=bank[:, q, :], in_=words[:, first : first + P], identity=ident[:])
+            dst = grouped_of[i][:].bitcast(F32)[:, b * 512 : (b + 1) * 512]
+            if kind == "w" and h == WHOLE:
+                nc.scalar.copy(out=dst.rearrange("p (j q) -> p j q", q=4), in_=bank[:].rearrange("p q j -> p j q"))
             else:
+                dst = dst.rearrange("p (s j u) -> p s j u", s=2, u=2)
+                src = bank[:].rearrange("p (s u) j -> p s j u", s=2)
+                if kind == "x" and b in X_VECTOR_BANKS:
+                    nc.vector.tensor_copy(out=dst, in_=src)
+                else:
+                    nc.scalar.copy(out=dst, in_=src)
+
+        def quantise(i, b):
+            kind, n, h = units[i]
+            if kind == "x":
+                codes, scales = x_codes[:, n, :], x_scales[:, n, :]
+            else:
+                codes, scales = w_quantised[n][0][:], w_quantised[n][1][:]
+            grouped = grouped_of[i]
+            if b is None:
+                nc.vector.quantize_mx(out=codes.bitcast(FP8X4), scales=scales, in_=grouped[:])
+            elif h == WHOLE:
+                cs = slice(b * 256, (b + 1) * 256)
+                nc.vector.quantize_mx(out=codes[:, cs].bitcast(FP8X4), scales=scales[:, cs], in_=grouped[:, b * 1024 : (b + 1) * 1024])
+            else:
+                for g in (2 * b, 2 * b + 1):
+                    cs = slice(g * ROWS + h * P, g * ROWS + (h + 1) * P)
+                    nc.vector.quantize_mx(out=codes[:, cs].bitcast(FP8X4), scales=scales[:, cs], in_=grouped[:, g * 512 : (g + 1) * 512])
+
+        def prepare(i):
+            kind, n, h = units[i]
+            nb = n_banks(i)
+            grouped = grouped_pool.tile([P, nb * 1024], BF16, tag="grouped", align_bytes=64)
+            grouped_of[i] = grouped
+            if kind == "w" and n not in w_quantised:
                 w_codes = wq_pool.tile([P, PASSES * ROWS], U32, tag="w_codes", align_bytes=64)
                 w_scales = wq_pool.tile([P, PASSES * ROWS], U8, tag="w_scales", align_bytes=64)
                 w_quantised[n] = (w_codes, w_scales)
-                codes = w_codes[:]
-                scales = w_scales[:]
-            nc.vector.quantize_mx(out=codes.bitcast(FP8X4), scales=scales, in_=grouped[:])
+            ahead = i + 1 < len(units) and units[i + 1][0] == "w" and units[i + 1][1] >= AHEAD_FROM
+            if ahead:
+                apply_mask(i + 1, 4)
+            if is_fine(i):
+                for b in range(nb):
+                    apply_mask(i, 1)
+                    fill_bank(i, b)
+                    if b >= LAG:
+                        quantise(i, b - LAG)
+                for b in range(nb - LAG, nb):
+                    quantise(i, b)
+            else:
+                apply_mask(i, 1)
+                for b in range(nb):
+                    fill_bank(i, b)
+                quantise(i, None)
+            state[pool_of(i)] += 1
 
-        def cell(c, tp):
-            w_codes, w_scales = w_quantised[c]
-            acc = mx_psum.tile([P, 2, ROWS], F32, tag="mx")
+        def multiply(c, h, tp):
+            codes, scales = w_quantised[c]
+            if (c, tp) not in banks_open:
+                acc = mx_psum.tile([P, 2, ROWS], F32, tag="mx")
+                banks_open[(c, tp)] = acc
+            acc = banks_open[(c, tp)]
+            lo = 0 if h == WHOLE else h * P
+            hi = ROWS if h == WHOLE else (h + 1) * P
             for tt in range(2):
                 for g in range(PASSES):
                     xs = slice((2 * g + tt) * P, (2 * g + tt + 1) * P)
-                    ws = slice(g * ROWS, (g + 1) * ROWS)
+                    ws = slice(g * ROWS + lo, g * ROWS + hi)
                     nc.tensor.matmul_mx(
-                        out=acc[:, tt, :],
+                        out=acc[:, tt, lo:hi],
                         lhsT=x_codes[:, tp, xs].bitcast(FP8X4),
                         lhsT_scale=x_scales[:, tp, xs],
-                        rhs=w_codes[:, ws].bitcast(FP8X4),
-                        rhs_scale=w_scales[:, ws],
+                        rhs=codes[:, ws].bitcast(FP8X4),
+                        rhs_scale=scales[:, ws],
                         start=(g == 0),
                         stop=(g == PASSES - 1),
                     )
+            if h == 0:
+                return
             gi = group_of[c]
             chunks = STORE_GROUPS[gi]
             part = c - chunks[0]
-            width = len(chunks) * ROWS
+            wide = len(chunks) * ROWS
             if (gi, tp) not in staged:
-                result = stage_pool.tile([P, 2, width], F32, name="result_%d_%d" % (gi, tp))
+                result = stage_pool.tile([P, 2, wide], F32, name="result_%d_%d" % (gi, tp))
                 staged[(gi, tp)] = result
             result = staged[(gi, tp)]
             bias_cols = bias_all[:, c * ROWS : (c + 1) * ROWS].unsqueeze(1).to_broadcast([P, 2, ROWS])
             nc.vector.tensor_tensor(out=result[:, :, part * ROWS : (part + 1) * ROWS], in0=acc[:], in1=bias_cols, op=ADD)
             if c == chunks[-1]:
                 first = chunks[0] * ROWS
-                nc.sync.dma_start(out=out_rows[:, 2 * tp : 2 * tp + 2, first : first + width], in_=result[:])
+                nc.sync.dma_start(out=out_rows[:, 2 * tp : 2 * tp + 2, first : first + wide], in_=result[:])
 
-        def is_early(i):
-            return i < len(items) and items[i][0] == "w" and items[i][1] >= EARLY_MASK_FROM
-
-        have = {"x": [], "w": []}
+        have_x = []
+        have_w = []
         pending = []
-        apply_mask(0)
-        for i in range(len(items)):
-            if is_early(i + 1):
-                apply_mask(i + 1)
-            grouped = transposes(i)
+        for i in range(len(units)):
+            prepare(i)
             load_more()
-            quantise(i, grouped)
-            if i == 1:
-                spread_bias()
-            for c, tp in pending:
-                cell(c, tp)
-            if i + 1 < len(items) and not is_early(i + 1):
-                apply_mask(i + 1)
-            kind, n = items[i]
+            for b in BIAS_AT.get(i, []):
+                spread_bias(b)
+            for c, h, tp in pending:
+                multiply(c, h, tp)
+            kind, n, h = units[i]
             if kind == "x":
-                pending = [(c, n) for c in have["w"]]
+                pending = [(c, hh, n) for c, hh in have_w]
+                have_x.append(n)
+            elif n in NARROW:
+                pending = [(n, h, tp) for tp in have_x]
+                have_w.append((n, h))
+            elif h != 0:
+                pending = [(n, WHOLE, tp) for tp in have_x]
+                have_w.append((n, WHOLE))
             else:
-                pending = [(n, tp) for tp in have["x"]]
-            have[kind].append(n)
-        for c, tp in pending:
-            cell(c, tp)
+                pending = []
+        for c, h, tp in pending:
+            multiply(c, h, tp)

@@ -31,8 +31,9 @@ AHEAD_FROM = 1
 LAG = 1
 X_VECTOR_BANKS = [3]
 STORE_GROUPS = [[0, 1, 2, 3], [4, 5], [6], [7]]
-BIAS_AT = {0: [0, 1, 2, 3]}
-BIAS_VECTOR = []
+BIAS_AFTER = 0
+WARM_START = 6
+WARM = {1: 1, 2: 1}
 WHOLE = 2
 
 
@@ -108,16 +109,24 @@ def tile_sparselayer_kernel(tc, x, weights, bias, mask, out):
         load_more()
         ones = const.tile([P, P], BF16)
         nc.vector.memset(ones[:], 1.0)
-        bias_all = const.tile([P, FEAT], F32)
+        zeros = const.tile([P, 512], BF16)
+        nc.vector.memset(zeros[:], 0.0)
+        bias_all = const.tile([P, FEAT], BF16)
+        junk = mx_psum.tile([P, 512], F32, tag="mx")
 
-        def spread_bias(b):
-            cols = slice(b * 512, (b + 1) * 512)
-            spread = mx_psum.tile([P, 512], F32, tag="mx")
-            nc.tensor.matmul(out=spread[:], lhsT=ones[:], rhs=bias_row[:, cols], start=True, stop=True)
-            if b in BIAS_VECTOR:
-                nc.vector.tensor_copy(out=bias_all[:, cols], in_=spread[:])
-            else:
-                nc.scalar.copy(out=bias_all[:, cols], in_=spread[:])
+        def warm(count):
+            for r in range(count):
+                nc.tensor.matmul(out=junk[:], lhsT=ones[:], rhs=zeros[:], start=True, stop=True)
+
+        def spread_bias():
+            for b in range(FEAT // 1024):
+                spread = mx_psum.tile([P, 1024], BF16, tag="mx")
+                for hb in range(2):
+                    cols = slice(b * 1024 + hb * 512, b * 1024 + (hb + 1) * 512)
+                    nc.tensor.matmul(out=spread[:, hb * 512 : (hb + 1) * 512], lhsT=ones[:], rhs=bias_row[:, cols], start=True, stop=True)
+                nc.scalar.copy(out=bias_all[:, b * 1024 : (b + 1) * 1024], in_=spread[:])
+
+        warm(WARM_START)
 
         x_codes = const.tile([P, N_PIECES, PASSES * ROWS], U32, align_bytes=64)
         x_scales = const.tile([P, N_PIECES, PASSES * ROWS], U8, align_bytes=64)
@@ -218,6 +227,7 @@ def tile_sparselayer_kernel(tc, x, weights, bias, mask, out):
                 for b in range(nb):
                     apply_mask(i, 1)
                     fill_bank(i, b)
+                    warm(WARM.get(i, 0))
                     if b >= LAG:
                         quantise(i, b - LAG)
                 for b in range(nb - LAG, nb):
@@ -272,8 +282,8 @@ def tile_sparselayer_kernel(tc, x, weights, bias, mask, out):
         for i in range(len(units)):
             prepare(i)
             load_more()
-            for b in BIAS_AT.get(i, []):
-                spread_bias(b)
+            if i == BIAS_AFTER:
+                spread_bias()
             for c, h, tp in pending:
                 multiply(c, h, tp)
             kind, n, h = units[i]

@@ -29,12 +29,13 @@ NARROW = [1, 2]
 FINE_TO = 3
 AHEAD_FROM = 1
 LAG = 1
-X_VECTOR_BANKS = [3]
+X_VECTOR_BANKS = []
 STORE_GROUPS = [[0, 1, 2, 3], [4, 5], [6], [7]]
 BIAS_AFTER = 0
 WARM_START = 6
 WARM = {1: 1, 2: 1}
 WHOLE = 2
+SPLIT_CELLS = [(7, 3)]
 
 
 def tile_sparselayer_kernel(tc, x, weights, bias, mask, out):
@@ -239,7 +240,30 @@ def tile_sparselayer_kernel(tc, x, weights, bias, mask, out):
                 quantise(i, None)
             state[pool_of(i)] += 1
 
+        def multiply_split(c, tp):
+            codes, scales = w_quantised[c]
+            for tt in range(2):
+                small = mx_psum.tile([P, ROWS], F32, tag="mx")
+                for g in range(PASSES):
+                    xs = slice((2 * g + tt) * P, (2 * g + tt + 1) * P)
+                    ws = slice(g * ROWS, (g + 1) * ROWS)
+                    nc.tensor.matmul_mx(
+                        out=small[:],
+                        lhsT=x_codes[:, tp, xs].bitcast(FP8X4),
+                        lhsT_scale=x_scales[:, tp, xs],
+                        rhs=codes[:, ws].bitcast(FP8X4),
+                        rhs_scale=scales[:, ws],
+                        start=(g == 0),
+                        stop=(g == PASSES - 1),
+                    )
+                last = stage_pool.tile([P, ROWS], F32, name="last_%d_%d_%d" % (c, tp, tt))
+                nc.vector.tensor_tensor(out=last[:], in0=small[:], in1=bias_all[:, c * ROWS : (c + 1) * ROWS], op=ADD)
+                nc.sync.dma_start(out=out_rows[:, 2 * tp + tt, c * ROWS : (c + 1) * ROWS], in_=last[:])
+
         def multiply(c, h, tp):
+            if (c, tp) in SPLIT_CELLS:
+                multiply_split(c, tp)
+                return
             codes, scales = w_quantised[c]
             if (c, tp) not in banks_open:
                 acc = mx_psum.tile([P, 2, ROWS], F32, tag="mx")

from contextlib import ExitStack

import concourse.mybir as mybir
from concourse.masks import make_identity

F32 = mybir.dt.float32
BF16 = mybir.dt.bfloat16
U32 = mybir.dt.uint32
U8 = mybir.dt.uint8
FP8X4 = mybir.dt.float8_e4m3fn_x4
ADD = mybir.AluOpType.add
MULT = mybir.AluOpType.mult

P = 128
BATCH = 1024
K = 2048
FEAT = 2048
FLOPS = 2 * BATCH * K * FEAT

PASSES = K // 512
ROWS = 256
WORDS = K // 2
N_PIECES = BATCH // ROWS
N_CHUNKS = FEAT // ROWS
RAW_BUFS = 8
HALF_BUFS = 8
HALF_CHUNKS = 3
NARROW = [1, 2]
FINE_TO = 3
AHEAD_FROM = 1
LAG = 1
X_VECTOR_BANKS = []
STORE_GROUPS = [[0, 1, 2, 3], [4, 5], [6], [7]]
BIAS_AFTER = 0
WARM_START = 6
WARM = {1: 1, 2: 1}
WHOLE = 2
SPLIT_CELLS = [(7, 3)]


def tile_sparselayer_kernel(tc, x, weights, bias, mask, out):
    nc = tc.nc
    x_rows = x.rearrange("(p t) k -> p (t k)", t=BATCH // P)
    out_rows = out.rearrange("(p t) n -> p t n", t=BATCH // P)

    def w_units(c):
        if c < HALF_CHUNKS:
            return [("w", c, 0), ("w", c, 1)]
        return [("w", c, WHOLE)]

    units = w_units(0) + [("x", tp, WHOLE) for tp in range(N_PIECES)]
    for c in range(1, N_CHUNKS):
        units.extend(w_units(c))
    group_of = {}
    for gi, chunks in enumerate(STORE_GROUPS):
        for c in chunks:
            group_of[c] = gi

    with ExitStack() as ctx:
        const = ctx.enter_context(tc.tile_pool(name="const", bufs=1))
        raw_pool = ctx.enter_context(tc.tile_pool(name="raw", bufs=RAW_BUFS))
        half_pool = ctx.enter_context(tc.tile_pool(name="half", bufs=HALF_BUFS))
        grouped_pool = ctx.enter_context(tc.tile_pool(name="grouped", bufs=2))
        wq_pool = ctx.enter_context(tc.tile_pool(name="wq", bufs=3))
        stage_pool = ctx.enter_context(tc.tile_pool(name="stage", bufs=1))
        tp_psum = ctx.enter_context(tc.psum_pool(name="tp", bufs=4))
        mx_psum = ctx.enter_context(tc.psum_pool(name="mx", bufs=4))

        ident = const.tile([P, P], F32)
        make_identity(nc, ident[:])

        ctx.enter_context(tc.manual_schedule())

        raw = {}
        state = {"next_load": 0, "raw": RAW_BUFS, "half": HALF_BUFS}
        bias_row = const.tile([P, FEAT], BF16)
        nc.vector.memset(bias_row[:], 0.0)

        def load_more():
            while state["next_load"] < len(units):
                i = state["next_load"]
                kind, n, h = units[i]
                pool_name = "raw" if h == WHOLE else "half"
                need = 1 if kind == "x" else 2
                if state[pool_name] < need:
                    return
                state[pool_name] -= need
                state["next_load"] += 1
                if i == 1:
                    nc.sync.dma_start(out=bias_row[0:1, :], in_=bias.rearrange("(o n) -> o n", o=1))
                if kind == "x":
                    x_raw = raw_pool.tile([P, 2 * K], BF16, tag="raw")
                    nc.sync.dma_start(out=x_raw[:], in_=x_rows[:, n * 2 * K : (n + 1) * 2 * K])
                    raw[i] = (x_raw, None)
                elif h == WHOLE:
                    rows = slice(n * ROWS, (n + 1) * ROWS)
                    w_raw = raw_pool.tile([P, 2 * K], BF16, tag="raw")
                    nc.sync.dma_start(out=w_raw[:], in_=weights[rows, :].rearrange("(p s) k -> p (s k)", s=2))
                    m_raw = raw_pool.tile([P, 2 * K], BF16, tag="raw")
                    nc.sync.dma_start(out=m_raw[:], in_=mask[rows, :].rearrange("(p s) k -> p (s k)", s=2))
                    raw[i] = (w_raw, m_raw)
                else:
                    rows = slice(n * ROWS + h * P, n * ROWS + (h + 1) * P)
                    w_raw = half_pool.tile([P, K], BF16, tag="half")
                    nc.sync.dma_start(out=w_raw[:], in_=weights[rows, :])
                    m_raw = half_pool.tile([P, K], BF16, tag="half")
                    nc.sync.dma_start(out=m_raw[:], in_=mask[rows, :])
                    raw[i] = (w_raw, m_raw)

        load_more()
        ones = const.tile([P, P], BF16)
        nc.vector.memset(ones[:], 1.0)
        zeros = const.tile([P, 512], BF16)
        nc.vector.memset(zeros[:], 0.0)
        bias_all = const.tile([P, FEAT], BF16)
        junk = mx_psum.tile([P, 512], F32, tag="mx")

        def warm(count):
            for r in range(count):
                nc.tensor.matmul(out=junk[:], lhsT=ones[:], rhs=zeros[:], start=True, stop=True)

        def spread_bias():
            for b in range(FEAT // 1024):
                spread = mx_psum.tile([P, 1024], BF16, tag="mx")
                for hb in range(2):
                    cols = slice(b * 1024 + hb * 512, b * 1024 + (hb + 1) * 512)
                    nc.tensor.matmul(out=spread[:, hb * 512 : (hb + 1) * 512], lhsT=ones[:], rhs=bias_row[:, cols], start=True, stop=True)
                nc.scalar.copy(out=bias_all[:, b * 1024 : (b + 1) * 1024], in_=spread[:])

        warm(WARM_START)

        x_codes = const.tile([P, N_PIECES, PASSES * ROWS], U32, align_bytes=64)
        x_scales = const.tile([P, N_PIECES, PASSES * ROWS], U8, align_bytes=64)
        w_quantised = {}
        grouped_of = {}
        staged = {}
        banks_open = {}
        mask_parts = {}

        def n_banks(i):
            return 4 if units[i][2] == WHOLE else 2

        def is_fine(i):
            kind, n, h = units[i]
            return kind == "x" or n <= FINE_TO

        def pool_of(i):
            return "raw" if units[i][2] == WHOLE else "half"

        for i in range(len(units)):
            if units[i][0] == "w":
                mask_parts[i] = n_banks(i) if is_fine(i) else 1

        def apply_mask(i, count):
            if i >= len(units) or units[i][0] == "x":
                return
            kind, n, h = units[i]
            w_raw, m_raw = raw[i]
            for r in range(count):
                if mask_parts[i] == 0:
                    return
                b = n_banks(i) - mask_parts[i]
                mask_parts[i] -= 1
                if not is_fine(i):
                    nc.vector.tensor_tensor(out=w_raw[:], in0=w_raw[:], in1=m_raw[:], op=MULT)
                elif h == WHOLE:
                    ks = slice(b * 512, (b + 1) * 512)
                    w3 = w_raw[:].rearrange("p (s k) -> p s k", s=2)
                    m3 = m_raw[:].rearrange("p (s k) -> p s k", s=2)
                    nc.vector.tensor_tensor(out=w3[:, :, ks], in0=w3[:, :, ks], in1=m3[:, :, ks], op=MULT)
                else:
                    ks = slice(b * 1024, (b + 1) * 1024)
                    nc.vector.tensor_tensor(out=w_raw[:, ks], in0=w_raw[:, ks], in1=m_raw[:, ks], op=MULT)
                if mask_parts[i] == 0:
                    state[pool_of(i)] += 1

        def fill_bank(i, b):
            kind, n, h = units[i]
            words = raw[i][0][:].bitcast(F32)
            bank = tp_psum.tile([P, 4, P], F32, tag="tp")
            for q in range(4):
                if h == WHOLE:
                    first = (q // 2) * WORDS + (2 * b + q % 2) * P
                else:
                    first = (4 * b + q) * P
                nc.tensor.transpose(out=bank[:, q, :], in_=words[:, first : first + P], identity=ident[:])
            dst = grouped_of[i][:].bitcast(F32)[:, b * 512 : (b + 1) * 512]
            if kind == "w" and h == WHOLE:
                nc.scalar.copy(out=dst.rearrange("p (j q) -> p j q", q=4), in_=bank[:].rearrange("p q j -> p j q"))
            else:
                dst = dst.rearrange("p (s j u) -> p s j u", s=2, u=2)
                src = bank[:].rearrange("p (s u) j -> p s j u", s=2)
                if kind == "x" and b in X_VECTOR_BANKS:
                    nc.vector.tensor_copy(out=dst, in_=src)
                else:
                    nc.scalar.copy(out=dst, in_=src)

        def quantise(i, b):
            kind, n, h = units[i]
            if kind == "x":
                codes, scales = x_codes[:, n, :], x_scales[:, n, :]
            else:
                codes, scales = w_quantised[n][0][:], w_quantised[n][1][:]
            grouped = grouped_of[i]
            if b is None:
                nc.vector.quantize_mx(out=codes.bitcast(FP8X4), scales=scales, in_=grouped[:])
            elif h == WHOLE:
                cs = slice(b * 256, (b + 1) * 256)
                nc.vector.quantize_mx(out=codes[:, cs].bitcast(FP8X4), scales=scales[:, cs], in_=grouped[:, b * 1024 : (b + 1) * 1024])
            else:
                for g in (2 * b, 2 * b + 1):
                    cs = slice(g * ROWS + h * P, g * ROWS + (h + 1) * P)
                    nc.vector.quantize_mx(out=codes[:, cs].bitcast(FP8X4), scales=scales[:, cs], in_=grouped[:, g * 512 : (g + 1) * 512])

        def prepare(i):
            kind, n, h = units[i]
            nb = n_banks(i)
            grouped = grouped_pool.tile([P, nb * 1024], BF16, tag="grouped", align_bytes=64)
            grouped_of[i] = grouped
            if kind == "w" and n not in w_quantised:
                w_codes = wq_pool.tile([P, PASSES * ROWS], U32, tag="w_codes", align_bytes=64)
                w_scales = wq_pool.tile([P, PASSES * ROWS], U8, tag="w_scales", align_bytes=64)
                w_quantised[n] = (w_codes, w_scales)
            ahead = i + 1 < len(units) and units[i + 1][0] == "w" and units[i + 1][1] >= AHEAD_FROM
            if ahead:
                apply_mask(i + 1, 4)
            if is_fine(i):
                for b in range(nb):
                    apply_mask(i, 1)
                    fill_bank(i, b)
                    warm(WARM.get(i, 0))
                    if b >= LAG:
                        quantise(i, b - LAG)
                for b in range(nb - LAG, nb):
                    quantise(i, b)
            else:
                apply_mask(i, 1)
                for b in range(nb):
                    fill_bank(i, b)
                quantise(i, None)
            state[pool_of(i)] += 1

        def multiply_split(c, tp):
            codes, scales = w_quantised[c]
            for tt in range(2):
                small = mx_psum.tile([P, ROWS], F32, tag="mx")
                for g in range(PASSES):
                    xs = slice((2 * g + tt) * P, (2 * g + tt + 1) * P)
                    ws = slice(g * ROWS, (g + 1) * ROWS)
                    nc.tensor.matmul_mx(
                        out=small[:],
                        lhsT=x_codes[:, tp, xs].bitcast(FP8X4),
                        lhsT_scale=x_scales[:, tp, xs],
                        rhs=codes[:, ws].bitcast(FP8X4),
                        rhs_scale=scales[:, ws],
                        start=(g == 0),
                        stop=(g == PASSES - 1),
                    )
                last = stage_pool.tile([P, ROWS], F32, name="last_%d_%d_%d" % (c, tp, tt))
                nc.vector.tensor_tensor(out=last[:], in0=small[:], in1=bias_all[:, c * ROWS : (c + 1) * ROWS], op=ADD)
                nc.sync.dma_start(out=out_rows[:, 2 * tp + tt, c * ROWS : (c + 1) * ROWS], in_=last[:])

        def multiply(c, h, tp):
            if (c, tp) in SPLIT_CELLS:
                multiply_split(c, tp)
                return
            codes, scales = w_quantised[c]
            if (c, tp) not in banks_open:
                acc = mx_psum.tile([P, 2, ROWS], F32, tag="mx")
                banks_open[(c, tp)] = acc
            acc = banks_open[(c, tp)]
            lo = 0 if h == WHOLE else h * P
            hi = ROWS if h == WHOLE else (h + 1) * P
            for tt in range(2):
                for g in range(PASSES):
                    xs = slice((2 * g + tt) * P, (2 * g + tt + 1) * P)
                    ws = slice(g * ROWS + lo, g * ROWS + hi)
                    nc.tensor.matmul_mx(
                        out=acc[:, tt, lo:hi],
                        lhsT=x_codes[:, tp, xs].bitcast(FP8X4),
                        lhsT_scale=x_scales[:, tp, xs],
                        rhs=codes[:, ws].bitcast(FP8X4),
                        rhs_scale=scales[:, ws],
                        start=(g == 0),
                        stop=(g == PASSES - 1),
                    )
            if h == 0:
                return
            gi = group_of[c]
            chunks = STORE_GROUPS[gi]
            part = c - chunks[0]
            wide = len(chunks) * ROWS
            if (gi, tp) not in staged:
                result = stage_pool.tile([P, 2, wide], F32, name="result_%d_%d" % (gi, tp))
                staged[(gi, tp)] = result
            result = staged[(gi, tp)]
            bias_cols = bias_all[:, c * ROWS : (c + 1) * ROWS].unsqueeze(1).to_broadcast([P, 2, ROWS])
            nc.vector.tensor_tensor(out=result[:, :, part * ROWS : (part + 1) * ROWS], in0=acc[:], in1=bias_cols, op=ADD)
            if c == chunks[-1]:
                first = chunks[0] * ROWS
                nc.sync.dma_start(out=out_rows[:, 2 * tp : 2 * tp + 2, first : first + wide], in_=result[:])

        have_x = []
        have_w = []
        pending = []
        for i in range(len(units)):
            prepare(i)
            load_more()
            if i == BIAS_AFTER:
                spread_bias()
            for c, h, tp in pending:
                multiply(c, h, tp)
            kind, n, h = units[i]
            if kind == "x":
                pending = [(c, hh, n) for c, hh in have_w]
                have_x.append(n)
            elif n in NARROW:
                pending = [(n, h, tp) for tp in have_x]
                have_w.append((n, h))
            elif h != 0:
                pending = [(n, WHOLE, tp) for tp in have_x]
                have_w.append((n, WHOLE))
            else:
                pending = []
        for c, h, tp in pending:
            multiply(c, h, tp)
